import numpy as np
import ml_dtypes


def mxq(x, axis, fmt="e4m3"):
    dtype, down = {"e4m3": (ml_dtypes.float8_e4m3fn, 7), "e5m2": (ml_dtypes.float8_e5m2, 14)}[fmt]
    v = np.moveaxis(np.asarray(x, np.float32).astype(ml_dtypes.bfloat16).astype(np.float64), axis, -1)
    blocks = v.reshape(v.shape[:-1] + (-1, 32))
    amax = np.abs(blocks).max(-1, keepdims=True)
    byte = np.maximum(np.where(amax > 0, np.frexp(amax)[1] - 1 + 127, 0) - down, 1)
    scale = np.exp2(byte - 127.0)
    codes = (blocks / scale).astype(np.float32).astype(dtype).astype(np.float64)
    return np.moveaxis((codes * scale).reshape(v.shape), -1, axis)


WIDE = False


def mx_kscale(k):
    if not WIDE:
        return np.ones(k)
    levels = np.array([10, -10, 5, -5, 0])
    if k % 512:
        return np.exp2(np.random.permutation(np.resize(levels, k // 32))).repeat(32)
    a = np.empty((k // 512, 16))
    for p in range(k // 512):
        a[p, :8] = np.random.permutation(np.resize(levels, 8))
        for g in range(8):
            far = levels[np.abs(levels - a[p, g]) >= 10]
            a[p, g + 8] = far[np.random.randint(len(far))]
    return np.exp2(a.ravel()).repeat(32)


BF16 = ml_dtypes.bfloat16


def bf(x):
    return np.asarray(x, np.float32).astype(BF16)


def f64(x):
    return np.asarray(x).astype(np.float64)


B, N, D0, D1, D2, D3 = 64, 128, 512, 512, 512, 1024
EPS = 1e-5


def batch_norm(x, g, b):
    mean = x.mean(axis=(0, 1))
    var = np.square(x - mean).mean(axis=(0, 1))
    return (x - mean) * (1.0 / np.sqrt(var + EPS)) * g + b


def setup_inputs():
    s = mx_kscale(D0)
    feats = np.random.standard_normal((B, N, D0)) * np.exp(0.4 * np.random.standard_normal(D0)) + 0.5 * np.random.standard_normal(D0)
    return {"set_feats": bf(feats),
            "g0": bf((1.0 + 0.2 * np.random.standard_normal(D0)) * s),
            "b0": bf(0.2 * np.random.standard_normal(D0) * s),
            "W0": bf(np.random.standard_normal((D1, D0)) / np.sqrt(D0) / s),
            "c0": bf(0.3 * np.random.standard_normal(D1)),
            "g1": bf(1.0 + 0.2 * np.random.standard_normal(D1)),
            "b1": bf(0.2 * np.random.standard_normal(D1))}


def reference(set_feats, g0, b0, W0, c0, g1, b1):
    x0 = batch_norm(f64(set_feats), f64(g0), f64(b0))
    h0 = np.maximum((mxq(x0, 2, "e4m3") @ mxq(f64(W0), 1, "e4m3").T) + f64(c0), 0.0)
    return batch_norm(h0, f64(g1), f64(b1))

@@ -1,0 +1,278 @@
+import concourse.mybir as mybir
+from concourse.masks import make_identity
+
+F32 = mybir.dt.float32
+BF16 = mybir.dt.bfloat16
+U32 = mybir.dt.uint32
+U8 = mybir.dt.uint8
+FP8X4 = mybir.dt.float8_e4m3fn_x4
+ALU = mybir.AluOpType
+FUNC = mybir.ActivationFunctionType
+
+P = 128
+PACK = 4
+ROWS = 64 * 128
+D_IN = 512
+D_OUT = 512
+EPS = 1e-5
+BLOCKS = 4
+ROWS_PER_PARTITION = ROWS // P
+CHUNK = 512
+SLICES = CHUNK // P
+CHUNKS = ROWS // CHUNK
+STATS = 6
+CHUNKS_BEFORE_W = 2
+VECTOR_BLOCKS = 2
+SCALAR_BLOCKS = BLOCKS - VECTOR_BLOCKS
+
+FLOPS = 2 * ROWS * D_IN * D_OUT
+
+
+def norm_coefficients(nc, pool, mean_var, gain, shift, label):
+    mean = mean_var[:, :, 0]
+    var_eps = pool.tile([P, BLOCKS], F32, name=label + "_var_eps")
+    nc.vector.tensor_scalar_add(out=var_eps[:], in0=mean_var[:, :, 1], scalar1=EPS)
+    rstd = pool.tile([P, BLOCKS], F32, name=label + "_rstd")
+    nc.scalar.sqrt(out=rstd[:], in_=var_eps[:])
+    nc.vector.reciprocal(out=rstd[:], in_=rstd[:])
+    newton = pool.tile([P, BLOCKS], F32, name=label + "_newton")
+    nc.vector.tensor_mul(out=newton[:], in0=rstd[:], in1=rstd[:])
+    nc.vector.tensor_mul(out=newton[:], in0=newton[:], in1=var_eps[:])
+    nc.vector.tensor_scalar(
+        out=newton[:], in0=newton[:], scalar1=-0.5, scalar2=1.5, op0=ALU.mult, op1=ALU.add
+    )
+    nc.vector.tensor_mul(out=rstd[:], in0=rstd[:], in1=newton[:])
+    scale = pool.tile([P, BLOCKS], F32, name=label + "_scale")
+    nc.vector.tensor_mul(out=scale[:], in0=rstd[:], in1=gain)
+    offset = pool.tile([P, BLOCKS], F32, name=label + "_offset")
+    nc.vector.tensor_mul(out=offset[:], in0=mean, in1=scale[:])
+    nc.vector.tensor_sub(out=offset[:], in0=shift, in1=offset[:])
+    return scale, offset
+
+
+def tile_settransform_pa_kernel(tc, set_feats, g0, b0, W0, c0, g1, b1, out):
+    nc = tc.nc
+    x_rows = set_feats.flatten_outer_dims().rearrange("(p c) k -> p c k", c=ROWS_PER_PARTITION)
+    out_rows = out.flatten_outer_dims().rearrange("(p c) f -> p c f", c=ROWS_PER_PARTITION)
+
+    with tc.tile_pool(name="keep", bufs=1) as keep:
+        ident_bf16 = keep.tile([P, P], BF16, name="ident_bf16")
+        make_identity(nc, ident_bf16[:])
+        ident_f32 = keep.tile([P, P], F32, name="ident_f32")
+        make_identity(nc, ident_f32[:])
+        warm = keep.tile([P, 1], F32, name="warm")
+        nc.vector.memset(warm[:], 1.0)
+        nc.scalar.sqrt(out=warm[:], in_=warm[:])
+
+        w_codes = keep.tile([P, D_OUT], U32, name="w_codes", align_bytes=64)
+        w_scales = keep.tile([P, D_OUT], U8, name="w_scales", align_bytes=64)
+        params = keep.tile([P, 5 * BLOCKS], F32, name="params")
+        stats0 = keep.tile([P, BLOCKS, CHUNKS, STATS], F32, name="stats0")
+        stats1 = keep.tile([P, VECTOR_BLOCKS, CHUNKS, STATS], F32, name="stats1")
+        sum_h = keep.tile([P, SCALAR_BLOCKS, CHUNKS], F32, name="sum_h")
+        sum_sq = keep.tile([P, SCALAR_BLOCKS, CHUNKS], F32, name="sum_sq")
+        neg_shift = keep.tile([P, SCALAR_BLOCKS], F32, name="neg_shift")
+        xt = [keep.tile([P, BLOCKS, CHUNK], BF16, name="xt%d" % j) for j in range(CHUNKS)]
+
+        with tc.tile_pool(name="natural", bufs=1) as natural, tc.psum_pool(
+            name="turned", bufs=6
+        ) as turned_pool:
+            x_nat = [natural.tile([P, SLICES, D_IN], BF16, name="x_nat%d" % j) for j in range(CHUNKS)]
+            w_nat = natural.tile([P, BLOCKS, D_IN], BF16, name="w_nat")
+            for j in range(CHUNKS):
+                if j == CHUNKS_BEFORE_W:
+                    nc.sync.dma_start(out=w_nat[:], in_=W0.rearrange("(b f) k -> f b k", f=P))
+                nc.sync.dma_start(
+                    out=x_nat[j][:], in_=x_rows[:, j * SLICES : (j + 1) * SLICES, :]
+                )
+            vec_rows = natural.tile([P, P], BF16, name="vec_rows")
+            nc.vector.memset(vec_rows[:], 0.0)
+            for v, vec in enumerate((c0, g1, b1)):
+                nc.scalar.dma_start(
+                    out=vec_rows[BLOCKS * v : BLOCKS * (v + 1), :],
+                    in_=vec.rearrange("(t p) -> t p", p=P),
+                )
+            in_vecs = [natural.tile([P, PACK], BF16, name="in_vec%d" % v) for v in range(2)]
+            for v, vec in enumerate((g0, b0)):
+                nc.scalar.dma_start(
+                    out=in_vecs[v][:], in_=vec.rearrange("(p t) -> p t", t=PACK)
+                )
+
+            for j in range(CHUNKS):
+                if j == CHUNKS_BEFORE_W:
+                    w_grouped = natural.tile(
+                        [P, D_OUT, PACK], BF16, name="w_grouped", align_bytes=64
+                    )
+                    for block in range(BLOCKS):
+                        w_turned = turned_pool.tile([P, PACK, P], BF16, tag="turned")
+                        for t in range(PACK):
+                            nc.tensor.transpose(
+                                out=w_turned[:, t, :],
+                                in_=w_nat[:, block, t::PACK],
+                                identity=ident_bf16[:],
+                            )
+                        nc.scalar.copy(
+                            out=w_grouped[:, block * P : (block + 1) * P, :],
+                            in_=w_turned[:].rearrange("p t f -> p f t"),
+                        )
+                    nc.vector.quantize_mx(
+                        out=w_codes[:].bitcast(FP8X4),
+                        scales=w_scales[:],
+                        in_=w_grouped[:].rearrange("p f t -> p (f t)"),
+                    )
+                    vec_turned = turned_pool.tile([P, PACK, P], BF16, tag="turned")
+                    nc.tensor.transpose(
+                        out=vec_turned[:, 0, :], in_=vec_rows[:], identity=ident_bf16[:]
+                    )
+                    nc.vector.tensor_copy(
+                        out=params[:, 2 * BLOCKS :], in_=vec_turned[:, 0, 0 : 3 * BLOCKS]
+                    )
+                    for v in range(2):
+                        nc.vector.tensor_copy(
+                            out=params[:, v * BLOCKS : (v + 1) * BLOCKS], in_=in_vecs[v][:]
+                        )
+                for s in range(SLICES):
+                    x_turned = turned_pool.tile([P, PACK, P], BF16, tag="turned")
+                    for t in range(PACK):
+                        nc.tensor.transpose(
+                            out=x_turned[:, t, :],
+                            in_=x_nat[j][:, s, t::PACK],
+                            identity=ident_bf16[:],
+                        )
+                    nc.scalar.copy(out=xt[j][:, :, s * P : (s + 1) * P], in_=x_turned[:])
+                for t in range(PACK):
+                    nc.vector.bn_stats(out=stats0[:, t, j, :], in_=xt[j][:, t, :])
+
+        mean_var0 = keep.tile([P, BLOCKS, 2], F32, name="mean_var0")
+        for t in range(PACK):
+            nc.vector.bn_aggr(
+                out=mean_var0[:, t, :], in_=stats0[:, t, :, :].rearrange("p j s -> p (j s)")
+            )
+        scale0, offset0 = norm_coefficients(
+            nc, keep, mean_var0, params[:, 0:BLOCKS], params[:, BLOCKS : 2 * BLOCKS], "norm0"
+        )
+        bias = params[:, 2 * BLOCKS : 3 * BLOCKS]
+
+        with tc.tile_pool(name="hidden", bufs=1) as hidden:
+            h = [hidden.tile([P, BLOCKS, CHUNK], F32, name="h%d" % j) for j in range(CHUNKS)]
+
+            with tc.tile_pool(name="operand", bufs=3) as operand, tc.psum_pool(
+                name="sums", bufs=8
+            ) as sums_pool:
+                for j in range(CHUNKS):
+                    for t in range(PACK):
+                        nc.vector.tensor_scalar(
+                            out=xt[j][:, t, :],
+                            in0=xt[j][:, t, :],
+                            scalar1=scale0[:, t : t + 1],
+                            scalar2=offset0[:, t : t + 1],
+                            op0=ALU.mult,
+                            op1=ALU.add,
+                        )
+                    grouped = operand.tile([P, CHUNK, PACK], BF16, name="grouped", align_bytes=64)
+                    grouped_view = grouped[:].rearrange("p (c i) t -> p c t i", i=4)
+                    planes_view = xt[j][:].rearrange("p t (c i) -> p c t i", i=4)
+                    nc.vector.tensor_copy(out=grouped_view, in_=planes_view)
+                    codes = operand.tile([P, CHUNK], U32, name="codes", align_bytes=64)
+                    scales = operand.tile([P, CHUNK], U8, name="scales", align_bytes=64)
+                    nc.vector.quantize_mx(
+                        out=codes[:].bitcast(FP8X4),
+                        scales=scales[:],
+                        in_=grouped[:].rearrange("p n t -> p (n t)"),
+                    )
+                    for block in range(BLOCKS):
+                        features = slice(block * P, (block + 1) * P)
+                        sums = sums_pool.tile([P, CHUNK], F32, name="sums")
+                        nc.tensor.matmul_mx(
+                            out=sums[:],
+                            lhsT=w_codes[:, features].bitcast(FP8X4),
+                            lhsT_scale=w_scales[:, features],
+                            rhs=codes[:].bitcast(FP8X4),
+                            rhs_scale=scales[:],
+                            start=True,
+                            stop=True,
+                        )
+                        if block < VECTOR_BLOCKS:
+                            nc.scalar.activation(
+                                out=h[j][:, block, :],
+                                in_=sums[:],
+                                func=FUNC.Relu,
+                                bias=bias[:, block : block + 1],
+                            )
+                            nc.vector.bn_stats(out=stats1[:, block, j, :], in_=h[j][:, block, :])
+                        else:
+                            nc.scalar.activation(
+                                out=h[j][:, block, :],
+                                in_=sums[:],
+                                func=FUNC.Relu,
+                                bias=bias[:, block : block + 1],
+                                accum_out=sum_h[:, block - VECTOR_BLOCKS, j : j + 1],
+                            )
+                    if j == 0:
+                        nc.scalar.mul(out=neg_shift[:], in_=sum_h[:, :, 0], mul=-1.0 / CHUNK)
+                    for b in range(SCALAR_BLOCKS):
+                        squares = operand.tile([P, CHUNK], F32, name="squares")
+                        nc.scalar.activation(
+                            out=squares[:],
+                            in_=h[j][:, VECTOR_BLOCKS + b, :],
+                            func=FUNC.Square,
+                            bias=neg_shift[:, b : b + 1],
+                            accum_out=sum_sq[:, b, j : j + 1],
+                        )
+
+            mean_var1 = keep.tile([P, BLOCKS, 2], F32, name="mean_var1")
+            for block in range(VECTOR_BLOCKS):
+                nc.vector.bn_aggr(
+                    out=mean_var1[:, block, :],
+                    in_=stats1[:, block, :, :].rearrange("p j s -> p (j s)"),
+                )
+            scalar_mean = mean_var1[:, VECTOR_BLOCKS:, 0]
+            total_h = keep.tile([P, SCALAR_BLOCKS], F32, name="total_h")
+            nc.vector.reduce_sum(out=total_h[:], in_=sum_h[:], axis=mybir.AxisListType.X)
+            total_sq = keep.tile([P, SCALAR_BLOCKS], F32, name="total_sq")
+            nc.vector.reduce_sum(out=total_sq[:], in_=sum_sq[:], axis=mybir.AxisListType.X)
+            nc.vector.tensor_scalar_mul(out=scalar_mean, in0=total_h[:], scalar1=1.0 / ROWS)
+            gap = keep.tile([P, SCALAR_BLOCKS], F32, name="gap")
+            nc.vector.tensor_add(out=gap[:], in0=scalar_mean, in1=neg_shift[:])
+            nc.vector.tensor_mul(out=gap[:], in0=gap[:], in1=gap[:])
+            nc.vector.scalar_tensor_tensor(
+                out=mean_var1[:, VECTOR_BLOCKS:, 1],
+                in0=total_sq[:],
+                scalar=1.0 / ROWS,
+                in1=gap[:],
+                op0=ALU.mult,
+                op1=ALU.subtract,
+            )
+            scale1, offset1 = norm_coefficients(
+                nc, keep, mean_var1, params[:, 3 * BLOCKS : 4 * BLOCKS], params[:, 4 * BLOCKS :], "norm1"
+            )
+
+            with tc.tile_pool(name="result", bufs=3) as result_pool, tc.psum_pool(
+                name="back", bufs=8
+            ) as back_pool:
+                for j in range(CHUNKS):
+                    for block in range(BLOCKS):
+                        nc.vector.tensor_scalar(
+                            out=h[j][:, block, :],
+                            in0=h[j][:, block, :],
+                            scalar1=scale1[:, block : block + 1],
+                            scalar2=offset1[:, block : block + 1],
+                            op0=ALU.mult,
+                            op1=ALU.add,
+                        )
+                    result = result_pool.tile([P, SLICES, D_OUT], F32, name="result")
+                    for s in range(SLICES):
+                        back = back_pool.tile([P, D_OUT], F32, name="back")
+                        for block in range(BLOCKS):
+                            nc.tensor.transpose(
+                                out=back[:, block * P : (block + 1) * P],
+                                in_=h[j][:, block, s * P : (s + 1) * P],
+                                identity=ident_f32[:],
+                            )
+                        if s == SLICES - 1:
+                            nc.vector.tensor_copy(out=result[:, s, :], in_=back[:])
+                        else:
+                            nc.scalar.copy(out=result[:, s, :], in_=back[:])
+                    nc.sync.dma_start(
+                        out=out_rows[:, j * SLICES : (j + 1) * SLICES, :], in_=result[:]
+                    )

@@ -21,6 +21,11 @@ CHUNK = 512
 SLICES = CHUNK // P
 CHUNKS = ROWS // CHUNK
 STATS = 6
+GRAM_CHUNKS = range(1, 12, 2)
+VECTOR_CHUNKS = [j for j in range(CHUNKS) if j not in GRAM_CHUNKS]
+GRAM_ROWS = len(GRAM_CHUNKS) * CHUNK
+GRAM_PITCH = D_IN + 16
+GRAM_COLS = P + 1
 CHUNKS_BEFORE_W = 2
 VECTOR_BLOCKS = 2
 SCALAR_BLOCKS = BLOCKS - VECTOR_BLOCKS
@@ -67,7 +72,10 @@ def tile_settransform_pa_kernel(tc, set_feats, g0, b0, W0, c0, g1, b1, out):
         w_codes = keep.tile([P, D_OUT], U32, name="w_codes", align_bytes=64)
         w_scales = keep.tile([P, D_OUT], U8, name="w_scales", align_bytes=64)
         params = keep.tile([P, 5 * BLOCKS], F32, name="params")
-        stats0 = keep.tile([P, BLOCKS, CHUNKS, STATS], F32, name="stats0")
+        gram_at = len(VECTOR_CHUNKS) * STATS
+        stats0 = keep.tile([P, BLOCKS, gram_at + 3], F32, name="stats0")
+        gram_sq = keep.tile([P, BLOCKS], F32, name="gram_sq")
+        gram_mean_sq = keep.tile([P, BLOCKS], F32, name="gram_mean_sq")
         stats1 = keep.tile([P, VECTOR_BLOCKS, CHUNKS, STATS], F32, name="stats1")
         sum_h = keep.tile([P, SCALAR_BLOCKS, CHUNKS], F32, name="sum_h")
         sum_sq = keep.tile([P, SCALAR_BLOCKS, CHUNKS], F32, name="sum_sq")
@@ -75,15 +83,24 @@ def tile_settransform_pa_kernel(tc, set_feats, g0, b0, W0, c0, g1, b1, out):
         xt = [keep.tile([P, BLOCKS, CHUNK], BF16, name="xt%d" % j) for j in range(CHUNKS)]
 
         with tc.tile_pool(name="natural", bufs=1) as natural, tc.psum_pool(
-            name="turned", bufs=6
-        ) as turned_pool:
-            x_nat = [natural.tile([P, SLICES, D_IN], BF16, name="x_nat%d" % j) for j in range(CHUNKS)]
+            name="turned", bufs=4
+        ) as turned_pool, tc.psum_pool(name="gram", bufs=1) as gram_pool:
+            x_nat = []
+            for j in range(CHUNKS):
+                pitch = GRAM_PITCH if j in GRAM_CHUNKS else D_IN
+                x_tile = natural.tile([P, SLICES, pitch], BF16, name="x_nat%d" % j)
+                if j in GRAM_CHUNKS:
+                    nc.gpsimd.memset(x_tile[:, :, D_IN:], 1.0)
+                x_nat.append(x_tile)
+            gram = [gram_pool.tile([P, GRAM_COLS], F32, name="gram%d" % t) for t in range(PACK)]
+            diagonal = natural.tile([P, P], F32, name="diagonal")
+            nc.vector.memset(stats0[:, :, gram_at : gram_at + 1], float(GRAM_ROWS))
             w_nat = natural.tile([P, BLOCKS, D_IN], BF16, name="w_nat")
             for j in range(CHUNKS):
                 if j == CHUNKS_BEFORE_W:
                     nc.sync.dma_start(out=w_nat[:], in_=W0.rearrange("(b f) k -> f b k", f=P))
                 nc.sync.dma_start(
-                    out=x_nat[j][:], in_=x_rows[:, j * SLICES : (j + 1) * SLICES, :]
+                    out=x_nat[j][:, :, 0:D_IN], in_=x_rows[:, j * SLICES : (j + 1) * SLICES, :]
                 )
             vec_rows = natural.tile([P, P], BF16, name="vec_rows")
             nc.vector.memset(vec_rows[:], 0.0)
@@ -128,7 +145,7 @@ def tile_settransform_pa_kernel(tc, set_feats, g0, b0, W0, c0, g1, b1, out):
                         out=params[:, 2 * BLOCKS :], in_=vec_turned[:, 0, 0 : 3 * BLOCKS]
                     )
                     for v in range(2):
-                        nc.vector.tensor_copy(
+                        nc.gpsimd.tensor_copy(
                             out=params[:, v * BLOCKS : (v + 1) * BLOCKS], in_=in_vecs[v][:]
                         )
                 for s in range(SLICES):
@@ -136,17 +153,57 @@ def tile_settransform_pa_kernel(tc, set_feats, g0, b0, W0, c0, g1, b1, out):
                     for t in range(PACK):
                         nc.tensor.transpose(
                             out=x_turned[:, t, :],
-                            in_=x_nat[j][:, s, t::PACK],
+                            in_=x_nat[j][:, s, t:D_IN:PACK],
                             identity=ident_bf16[:],
                         )
                     nc.scalar.copy(out=xt[j][:, :, s * P : (s + 1) * P], in_=x_turned[:])
-                for t in range(PACK):
-                    nc.vector.bn_stats(out=stats0[:, t, j, :], in_=xt[j][:, t, :])
+                if j in GRAM_CHUNKS:
+                    for t in range(PACK):
+                        for s in range(SLICES):
+                            nc.tensor.matmul(
+                                out=gram[t][:],
+                                lhsT=x_nat[j][:, s, t:D_IN:PACK],
+                                rhs=x_nat[j][:, s, t : D_IN + PACK : PACK],
+                                start=(j == GRAM_CHUNKS[0] and s == 0),
+                                stop=(j == GRAM_CHUNKS[-1] and s == SLICES - 1),
+                            )
+                else:
+                    at = VECTOR_CHUNKS.index(j) * STATS
+                    for t in range(PACK):
+                        nc.vector.bn_stats(
+                            out=stats0[:, t, at : at + STATS], in_=xt[j][:, t, :]
+                        )
+
+            for t in range(PACK):
+                nc.vector.scalar_tensor_tensor(
+                    out=diagonal[:],
+                    in0=gram[t][:, 0:P],
+                    scalar=1.0,
+                    in1=ident_f32[:],
+                    op0=ALU.mult,
+                    op1=ALU.mult,
+                    accum_out=gram_sq[:, t : t + 1],
+                )
+                nc.vector.tensor_scalar_mul(
+                    out=stats0[:, t, gram_at + 1 : gram_at + 2],
+                    in0=gram[t][:, P : P + 1],
+                    scalar1=1.0 / GRAM_ROWS,
+                )
+            gram_mean = stats0[:, :, gram_at + 1]
+            nc.vector.tensor_mul(out=gram_mean_sq[:], in0=gram_mean, in1=gram_mean)
+            nc.vector.scalar_tensor_tensor(
+                out=stats0[:, :, gram_at + 2],
+                in0=gram_mean_sq[:],
+                scalar=-float(GRAM_ROWS),
+                in1=gram_sq[:],
+                op0=ALU.mult,
+                op1=ALU.add,
+            )
 
         mean_var0 = keep.tile([P, BLOCKS, 2], F32, name="mean_var0")
         for t in range(PACK):
             nc.vector.bn_aggr(
-                out=mean_var0[:, t, :], in_=stats0[:, t, :, :].rearrange("p j s -> p (j s)")
+                out=mean_var0[:, t, :], in_=stats0[:, t, :]
             )
         scale0, offset0 = norm_coefficients(
             nc, keep, mean_var0, params[:, 0:BLOCKS], params[:, BLOCKS : 2 * BLOCKS], "norm0"

@@ -21,11 +21,16 @@ CHUNK = 512
 SLICES = CHUNK // P
 CHUNKS = ROWS // CHUNK
 STATS = 6
-GRAM_CHUNKS = range(1, 12, 2)
-VECTOR_CHUNKS = [j for j in range(CHUNKS) if j not in GRAM_CHUNKS]
-GRAM_ROWS = len(GRAM_CHUNKS) * CHUNK
+GRAM_PLANES = [
+    [(j // 2 + 1) % PACK, (j // 2 + 3) % PACK] if j % 2 == 0 else [(j // 2) % PACK]
+    for j in range(CHUNKS)
+]
+GRAM_OF = [[j for j in range(CHUNKS) if t in GRAM_PLANES[j]] for t in range(PACK)]
+VECTOR_OF = [[j for j in range(CHUNKS) if t not in GRAM_PLANES[j]] for t in range(PACK)]
+GRAM_ROWS = len(GRAM_OF[0]) * CHUNK
 GRAM_PITCH = D_IN + 16
 GRAM_COLS = P + 1
+WARM_UPS = 5
 CHUNKS_BEFORE_W = 2
 VECTOR_BLOCKS = 2
 SCALAR_BLOCKS = BLOCKS - VECTOR_BLOCKS
@@ -72,7 +77,7 @@ def tile_settransform_pa_kernel(tc, set_feats, g0, b0, W0, c0, g1, b1, out):
         w_codes = keep.tile([P, D_OUT], U32, name="w_codes", align_bytes=64)
         w_scales = keep.tile([P, D_OUT], U8, name="w_scales", align_bytes=64)
         params = keep.tile([P, 5 * BLOCKS], F32, name="params")
-        gram_at = len(VECTOR_CHUNKS) * STATS
+        gram_at = len(VECTOR_OF[0]) * STATS
         stats0 = keep.tile([P, BLOCKS, gram_at + 3], F32, name="stats0")
         gram_sq = keep.tile([P, BLOCKS], F32, name="gram_sq")
         gram_mean_sq = keep.tile([P, BLOCKS], F32, name="gram_mean_sq")
@@ -87,10 +92,8 @@ def tile_settransform_pa_kernel(tc, set_feats, g0, b0, W0, c0, g1, b1, out):
         ) as turned_pool, tc.psum_pool(name="gram", bufs=1) as gram_pool:
             x_nat = []
             for j in range(CHUNKS):
-                pitch = GRAM_PITCH if j in GRAM_CHUNKS else D_IN
-                x_tile = natural.tile([P, SLICES, pitch], BF16, name="x_nat%d" % j)
-                if j in GRAM_CHUNKS:
-                    nc.gpsimd.memset(x_tile[:, :, D_IN:], 1.0)
+                x_tile = natural.tile([P, SLICES, GRAM_PITCH], BF16, name="x_nat%d" % j)
+                nc.gpsimd.memset(x_tile[:, :, D_IN:], 1.0)
                 x_nat.append(x_tile)
             gram = [gram_pool.tile([P, GRAM_COLS], F32, name="gram%d" % t) for t in range(PACK)]
             diagonal = natural.tile([P, P], F32, name="diagonal")
@@ -113,6 +116,12 @@ def tile_settransform_pa_kernel(tc, set_feats, g0, b0, W0, c0, g1, b1, out):
             for v, vec in enumerate((g0, b0)):
                 nc.scalar.dma_start(
                     out=in_vecs[v][:], in_=vec.rearrange("(p t) -> p t", t=PACK)
+                )
+
+            warm_up = turned_pool.tile([P, P], F32, tag="turned")
+            for i in range(WARM_UPS):
+                nc.tensor.matmul(
+                    out=warm_up[:], lhsT=ident_f32[:], rhs=ident_f32[:], start=True, stop=True
                 )
 
             for j in range(CHUNKS):
@@ -148,28 +157,28 @@ def tile_settransform_pa_kernel(tc, set_feats, g0, b0, W0, c0, g1, b1, out):
                         nc.gpsimd.tensor_copy(
                             out=params[:, v * BLOCKS : (v + 1) * BLOCKS], in_=in_vecs[v][:]
                         )
-                for s in range(SLICES):
-                    x_turned = turned_pool.tile([P, PACK, P], BF16, tag="turned")
-                    for t in range(PACK):
+                for t in range(PACK):
+                    x_turned = turned_pool.tile([P, SLICES, P], BF16, tag="turned")
+                    for s in range(SLICES):
                         nc.tensor.transpose(
-                            out=x_turned[:, t, :],
+                            out=x_turned[:, s, :],
                             in_=x_nat[j][:, s, t:D_IN:PACK],
                             identity=ident_bf16[:],
                         )
-                    nc.scalar.copy(out=xt[j][:, :, s * P : (s + 1) * P], in_=x_turned[:])
-                if j in GRAM_CHUNKS:
-                    for t in range(PACK):
+                    nc.scalar.copy(
+                        out=xt[j][:, t, :], in_=x_turned[:].rearrange("p s n -> p (s n)")
+                    )
+                    if t in GRAM_PLANES[j]:
                         for s in range(SLICES):
                             nc.tensor.matmul(
                                 out=gram[t][:],
                                 lhsT=x_nat[j][:, s, t:D_IN:PACK],
                                 rhs=x_nat[j][:, s, t : D_IN + PACK : PACK],
-                                start=(j == GRAM_CHUNKS[0] and s == 0),
-                                stop=(j == GRAM_CHUNKS[-1] and s == SLICES - 1),
+                                start=(j == GRAM_OF[t][0] and s == 0),
+                                stop=(j == GRAM_OF[t][-1] and s == SLICES - 1),
                             )
-                else:
-                    at = VECTOR_CHUNKS.index(j) * STATS
-                    for t in range(PACK):
+                    else:
+                        at = VECTOR_OF[t].index(j) * STATS
                         nc.vector.bn_stats(
                             out=stats0[:, t, at : at + STATS], in_=xt[j][:, t, :]
                         )

@@ -34,6 +34,7 @@ WARM_UPS = 5
 CHUNKS_BEFORE_W = 2
 VECTOR_BLOCKS = 2
 SCALAR_BLOCKS = BLOCKS - VECTOR_BLOCKS
+LAG = 2
 
 FLOPS = 2 * ROWS * D_IN * D_OUT
 
@@ -225,7 +226,9 @@ def tile_settransform_pa_kernel(tc, set_feats, g0, b0, W0, c0, g1, b1, out):
             with tc.tile_pool(name="operand", bufs=3) as operand, tc.psum_pool(
                 name="sums", bufs=8
             ) as sums_pool:
-                for j in range(CHUNKS):
+                codes, scales, grouped = {}, {}, {}
+
+                def normalise(j):
                     for t in range(PACK):
                         nc.vector.tensor_scalar(
                             out=xt[j][:, t, :],
@@ -235,17 +238,26 @@ def tile_settransform_pa_kernel(tc, set_feats, g0, b0, W0, c0, g1, b1, out):
                             op0=ALU.mult,
                             op1=ALU.add,
                         )
-                    grouped = operand.tile([P, CHUNK, PACK], BF16, name="grouped", align_bytes=64)
-                    grouped_view = grouped[:].rearrange("p (c i) t -> p c t i", i=4)
-                    planes_view = xt[j][:].rearrange("p t (c i) -> p c t i", i=4)
-                    nc.vector.tensor_copy(out=grouped_view, in_=planes_view)
-                    codes = operand.tile([P, CHUNK], U32, name="codes", align_bytes=64)
-                    scales = operand.tile([P, CHUNK], U8, name="scales", align_bytes=64)
-                    nc.vector.quantize_mx(
-                        out=codes[:].bitcast(FP8X4),
-                        scales=scales[:],
-                        in_=grouped[:].rearrange("p n t -> p (n t)"),
+
+                def interleave(j):
+                    grouped[j] = operand.tile(
+                        [P, CHUNK, PACK], BF16, name="grouped", align_bytes=64
                     )
+                    nc.vector.tensor_copy(
+                        out=grouped[j][:].rearrange("p (c i) t -> p c t i", i=4),
+                        in_=xt[j][:].rearrange("p t (c i) -> p c t i", i=4),
+                    )
+
+                def quantise(j):
+                    codes[j] = operand.tile([P, CHUNK], U32, name="codes", align_bytes=64)
+                    scales[j] = operand.tile([P, CHUNK], U8, name="scales", align_bytes=64)
+                    nc.vector.quantize_mx(
+                        out=codes[j][:].bitcast(FP8X4),
+                        scales=scales[j][:],
+                        in_=grouped[j][:].rearrange("p n t -> p (n t)"),
+                    )
+
+                def multiply(j):
                     for block in range(BLOCKS):
                         features = slice(block * P, (block + 1) * P)
                         sums = sums_pool.tile([P, CHUNK], F32, name="sums")
@@ -253,8 +265,8 @@ def tile_settransform_pa_kernel(tc, set_feats, g0, b0, W0, c0, g1, b1, out):
                             out=sums[:],
                             lhsT=w_codes[:, features].bitcast(FP8X4),
                             lhsT_scale=w_scales[:, features],
-                            rhs=codes[:].bitcast(FP8X4),
-                            rhs_scale=scales[:],
+                            rhs=codes[j][:].bitcast(FP8X4),
+                            rhs_scale=scales[j][:],
                             start=True,
                             stop=True,
                         )
@@ -265,7 +277,6 @@ def tile_settransform_pa_kernel(tc, set_feats, g0, b0, W0, c0, g1, b1, out):
                                 func=FUNC.Relu,
                                 bias=bias[:, block : block + 1],
                             )
-                            nc.vector.bn_stats(out=stats1[:, block, j, :], in_=h[j][:, block, :])
                         else:
                             nc.scalar.activation(
                                 out=h[j][:, block, :],
@@ -285,6 +296,24 @@ def tile_settransform_pa_kernel(tc, set_feats, g0, b0, W0, c0, g1, b1, out):
                             bias=neg_shift[:, b : b + 1],
                             accum_out=sum_sq[:, b, j : j + 1],
                         )
+
+                def measure(j, block):
+                    nc.vector.bn_stats(out=stats1[:, block, j, :], in_=h[j][:, block, :])
+
+                with tc.manual_schedule():
+                    normalise(0)
+                    for j in range(CHUNKS + LAG):
+                        if j < CHUNKS:
+                            interleave(j)
+                        if j >= LAG:
+                            measure(j - LAG, 0)
+                        if j < CHUNKS:
+                            quantise(j)
+                            multiply(j)
+                        if j + 1 < CHUNKS:
+                            normalise(j + 1)
+                        if j >= LAG:
+                            measure(j - LAG, 1)
 
             mean_var1 = keep.tile([P, BLOCKS, 2], F32, name="mean_var1")
             for block in range(VECTOR_BLOCKS):

@@ -35,28 +35,33 @@ CHUNKS_BEFORE_W = 2
 VECTOR_BLOCKS = 2
 SCALAR_BLOCKS = BLOCKS - VECTOR_BLOCKS
 LAG = 2
+PIECES = [(0, slice(0, CHUNK // 2)), (0, slice(CHUNK // 2, CHUNK))] + [
+    (j, slice(0, CHUNK)) for j in range(1, CHUNKS)
+]
+WIDTHS = [columns.stop - columns.start for j, columns in PIECES]
 
 FLOPS = 2 * ROWS * D_IN * D_OUT
 
 
 def norm_coefficients(nc, pool, mean_var, gain, shift, label):
-    mean = mean_var[:, :, 0]
+    rstd = pool.tile([P, BLOCKS], F32, name=label + "_rstd")
+    nc.scalar.activation(
+        out=rstd[:], in_=mean_var[:, :, 1], func=FUNC.Abs_reciprocal_sqrt, bias=EPS
+    )
     var_eps = pool.tile([P, BLOCKS], F32, name=label + "_var_eps")
     nc.vector.tensor_scalar_add(out=var_eps[:], in0=mean_var[:, :, 1], scalar1=EPS)
-    rstd = pool.tile([P, BLOCKS], F32, name=label + "_rstd")
-    nc.scalar.sqrt(out=rstd[:], in_=var_eps[:])
-    nc.vector.reciprocal(out=rstd[:], in_=rstd[:])
     newton = pool.tile([P, BLOCKS], F32, name=label + "_newton")
     nc.vector.tensor_mul(out=newton[:], in0=rstd[:], in1=rstd[:])
-    nc.vector.tensor_mul(out=newton[:], in0=newton[:], in1=var_eps[:])
-    nc.vector.tensor_scalar(
-        out=newton[:], in0=newton[:], scalar1=-0.5, scalar2=1.5, op0=ALU.mult, op1=ALU.add
-    )
-    nc.vector.tensor_mul(out=rstd[:], in0=rstd[:], in1=newton[:])
     scale = pool.tile([P, BLOCKS], F32, name=label + "_scale")
     nc.vector.tensor_mul(out=scale[:], in0=rstd[:], in1=gain)
+    nc.vector.scalar_tensor_tensor(
+        out=newton[:], in0=newton[:], scalar=-0.5, in1=var_eps[:], op0=ALU.mult, op1=ALU.mult
+    )
+    nc.vector.scalar_tensor_tensor(
+        out=scale[:], in0=newton[:], scalar=1.5, in1=scale[:], op0=ALU.add, op1=ALU.mult
+    )
     offset = pool.tile([P, BLOCKS], F32, name=label + "_offset")
-    nc.vector.tensor_mul(out=offset[:], in0=mean, in1=scale[:])
+    nc.vector.tensor_mul(out=offset[:], in0=mean_var[:, :, 0], in1=scale[:])
     nc.vector.tensor_sub(out=offset[:], in0=shift, in1=offset[:])
     return scale, offset
 
@@ -73,7 +78,7 @@ def tile_settransform_pa_kernel(tc, set_feats, g0, b0, W0, c0, g1, b1, out):
         make_identity(nc, ident_f32[:])
         warm = keep.tile([P, 1], F32, name="warm")
         nc.vector.memset(warm[:], 1.0)
-        nc.scalar.sqrt(out=warm[:], in_=warm[:])
+        nc.scalar.activation(out=warm[:], in_=warm[:], func=FUNC.Abs_reciprocal_sqrt)
 
         w_codes = keep.tile([P, D_OUT], U32, name="w_codes", align_bytes=64)
         w_scales = keep.tile([P, D_OUT], U8, name="w_scales", align_bytes=64)
@@ -83,7 +88,7 @@ def tile_settransform_pa_kernel(tc, set_feats, g0, b0, W0, c0, g1, b1, out):
         gram_sq = keep.tile([P, BLOCKS], F32, name="gram_sq")
         gram_mean_sq = keep.tile([P, BLOCKS], F32, name="gram_mean_sq")
         stats1 = keep.tile([P, VECTOR_BLOCKS, CHUNKS, STATS], F32, name="stats1")
-        sum_h = keep.tile([P, SCALAR_BLOCKS, CHUNKS], F32, name="sum_h")
+        sum_h = keep.tile([P, SCALAR_BLOCKS, len(PIECES)], F32, name="sum_h")
         sum_sq = keep.tile([P, SCALAR_BLOCKS, CHUNKS], F32, name="sum_sq")
         neg_shift = keep.tile([P, SCALAR_BLOCKS], F32, name="neg_shift")
         xt = [keep.tile([P, BLOCKS, CHUNK], BF16, name="xt%d" % j) for j in range(CHUNKS)]
@@ -166,10 +171,9 @@ def tile_settransform_pa_kernel(tc, set_feats, g0, b0, W0, c0, g1, b1, out):
                             in_=x_nat[j][:, s, t:D_IN:PACK],
                             identity=ident_bf16[:],
                         )
-                    nc.scalar.copy(
-                        out=xt[j][:, t, :], in_=x_turned[:].rearrange("p s n -> p (s n)")
-                    )
+                    turned = x_turned[:].rearrange("p s n -> p (s n)")
                     if t in GRAM_PLANES[j]:
+                        nc.vector.tensor_copy(out=xt[j][:, t, :], in_=turned)
                         for s in range(SLICES):
                             nc.tensor.matmul(
                                 out=gram[t][:],
@@ -179,6 +183,7 @@ def tile_settransform_pa_kernel(tc, set_feats, g0, b0, W0, c0, g1, b1, out):
                                 stop=(j == GRAM_OF[t][-1] and s == SLICES - 1),
                             )
                     else:
+                        nc.scalar.copy(out=xt[j][:, t, :], in_=turned)
                         at = VECTOR_OF[t].index(j) * STATS
                         nc.vector.bn_stats(
                             out=stats0[:, t, at : at + STATS], in_=xt[j][:, t, :]
@@ -228,92 +233,98 @@ def tile_settransform_pa_kernel(tc, set_feats, g0, b0, W0, c0, g1, b1, out):
             ) as sums_pool:
                 codes, scales, grouped = {}, {}, {}
 
-                def normalise(j):
+                def normalise(i):
+                    j, columns = PIECES[i]
                     for t in range(PACK):
                         nc.vector.tensor_scalar(
-                            out=xt[j][:, t, :],
-                            in0=xt[j][:, t, :],
+                            out=xt[j][:, t, columns],
+                            in0=xt[j][:, t, columns],
                             scalar1=scale0[:, t : t + 1],
                             scalar2=offset0[:, t : t + 1],
                             op0=ALU.mult,
                             op1=ALU.add,
                         )
 
-                def interleave(j):
-                    grouped[j] = operand.tile(
+                def interleave(i):
+                    j, columns = PIECES[i]
+                    grouped[i] = operand.tile(
                         [P, CHUNK, PACK], BF16, name="grouped", align_bytes=64
                     )
                     nc.vector.tensor_copy(
-                        out=grouped[j][:].rearrange("p (c i) t -> p c t i", i=4),
-                        in_=xt[j][:].rearrange("p t (c i) -> p c t i", i=4),
+                        out=grouped[i][:, 0 : WIDTHS[i], :].rearrange("p (c i) t -> p c t i", i=4),
+                        in_=xt[j][:, :, columns].rearrange("p t (c i) -> p c t i", i=4),
                     )
 
-                def quantise(j):
-                    codes[j] = operand.tile([P, CHUNK], U32, name="codes", align_bytes=64)
-                    scales[j] = operand.tile([P, CHUNK], U8, name="scales", align_bytes=64)
+                def quantise(i):
+                    codes[i] = operand.tile([P, CHUNK], U32, name="codes", align_bytes=64)
+                    scales[i] = operand.tile([P, CHUNK], U8, name="scales", align_bytes=64)
                     nc.vector.quantize_mx(
-                        out=codes[j][:].bitcast(FP8X4),
-                        scales=scales[j][:],
-                        in_=grouped[j][:].rearrange("p n t -> p (n t)"),
+                        out=codes[i][:, 0 : WIDTHS[i]].bitcast(FP8X4),
+                        scales=scales[i][:, 0 : WIDTHS[i]],
+                        in_=grouped[i][:, 0 : WIDTHS[i], :].rearrange("p n t -> p (n t)"),
                     )
 
-                def multiply(j):
+                def multiply(i):
+                    j, columns = PIECES[i]
                     for block in range(BLOCKS):
                         features = slice(block * P, (block + 1) * P)
                         sums = sums_pool.tile([P, CHUNK], F32, name="sums")
                         nc.tensor.matmul_mx(
-                            out=sums[:],
+                            out=sums[:, 0 : WIDTHS[i]],
                             lhsT=w_codes[:, features].bitcast(FP8X4),
                             lhsT_scale=w_scales[:, features],
-                            rhs=codes[j][:].bitcast(FP8X4),
-                            rhs_scale=scales[j][:],
+                            rhs=codes[i][:, 0 : WIDTHS[i]].bitcast(FP8X4),
+                            rhs_scale=scales[i][:, 0 : WIDTHS[i]],
                             start=True,
                             stop=True,
                         )
                         if block < VECTOR_BLOCKS:
                             nc.scalar.activation(
-                                out=h[j][:, block, :],
-                                in_=sums[:],
+                                out=h[j][:, block, columns],
+                                in_=sums[:, 0 : WIDTHS[i]],
                                 func=FUNC.Relu,
                                 bias=bias[:, block : block + 1],
                             )
                         else:
                             nc.scalar.activation(
-                                out=h[j][:, block, :],
-                                in_=sums[:],
+                                out=h[j][:, block, columns],
+                                in_=sums[:, 0 : WIDTHS[i]],
                                 func=FUNC.Relu,
                                 bias=bias[:, block : block + 1],
-                                accum_out=sum_h[:, block - VECTOR_BLOCKS, j : j + 1],
+                                accum_out=sum_h[:, block - VECTOR_BLOCKS, i : i + 1],
                             )
-                    if j == 0:
-                        nc.scalar.mul(out=neg_shift[:], in_=sum_h[:, :, 0], mul=-1.0 / CHUNK)
-                    for b in range(SCALAR_BLOCKS):
-                        squares = operand.tile([P, CHUNK], F32, name="squares")
-                        nc.scalar.activation(
-                            out=squares[:],
-                            in_=h[j][:, VECTOR_BLOCKS + b, :],
-                            func=FUNC.Square,
-                            bias=neg_shift[:, b : b + 1],
-                            accum_out=sum_sq[:, b, j : j + 1],
-                        )
+                    if i == 0:
+                        nc.scalar.mul(out=neg_shift[:], in_=sum_h[:, :, 0], mul=-1.0 / WIDTHS[0])
+                    if columns.stop == CHUNK:
+                        for b in range(SCALAR_BLOCKS):
+                            squares = operand.tile([P, CHUNK], F32, name="squares")
+                            nc.scalar.activation(
+                                out=squares[:],
+                                in_=h[j][:, VECTOR_BLOCKS + b, :],
+                                func=FUNC.Square,
+                                bias=neg_shift[:, b : b + 1],
+                                accum_out=sum_sq[:, b, j : j + 1],
+                            )
 
-                def measure(j, block):
-                    nc.vector.bn_stats(out=stats1[:, block, j, :], in_=h[j][:, block, :])
+                def measure(i, block):
+                    j, columns = PIECES[i]
+                    if columns.stop == CHUNK:
+                        nc.vector.bn_stats(out=stats1[:, block, j, :], in_=h[j][:, block, :])
 
                 with tc.manual_schedule():
                     normalise(0)
-                    for j in range(CHUNKS + LAG):
-                        if j < CHUNKS:
-                            interleave(j)
-                        if j >= LAG:
-                            measure(j - LAG, 0)
-                        if j < CHUNKS:
-                            quantise(j)
-                            multiply(j)
-                        if j + 1 < CHUNKS:
-                            normalise(j + 1)
-                        if j >= LAG:
-                            measure(j - LAG, 1)
+                    for i in range(len(PIECES) + LAG):
+                        if i < len(PIECES):
+                            interleave(i)
+                        if i >= LAG:
+                            measure(i - LAG, 0)
+                        if i < len(PIECES):
+                            quantise(i)
+                            multiply(i)
+                        if i + 1 < len(PIECES):
+                            normalise(i + 1)
+                        if i >= LAG:
+                            measure(i - LAG, 1)
 
             mean_var1 = keep.tile([P, BLOCKS, 2], F32, name="mean_var1")
             for block in range(VECTOR_BLOCKS):
@@ -326,9 +337,16 @@ def tile_settransform_pa_kernel(tc, set_feats, g0, b0, W0, c0, g1, b1, out):
             nc.vector.reduce_sum(out=total_h[:], in_=sum_h[:], axis=mybir.AxisListType.X)
             total_sq = keep.tile([P, SCALAR_BLOCKS], F32, name="total_sq")
             nc.vector.reduce_sum(out=total_sq[:], in_=sum_sq[:], axis=mybir.AxisListType.X)
-            nc.vector.tensor_scalar_mul(out=scalar_mean, in0=total_h[:], scalar1=1.0 / ROWS)
             gap = keep.tile([P, SCALAR_BLOCKS], F32, name="gap")
-            nc.vector.tensor_add(out=gap[:], in0=scalar_mean, in1=neg_shift[:])
+            nc.vector.scalar_tensor_tensor(
+                out=gap[:],
+                in0=total_h[:],
+                scalar=1.0 / ROWS,
+                in1=neg_shift[:],
+                op0=ALU.mult,
+                op1=ALU.add,
+            )
+            nc.vector.tensor_scalar_mul(out=scalar_mean, in0=total_h[:], scalar1=1.0 / ROWS)
             nc.vector.tensor_mul(out=gap[:], in0=gap[:], in1=gap[:])
             nc.vector.scalar_tensor_tensor(
                 out=mean_var1[:, VECTOR_BLOCKS:, 1],
@@ -345,18 +363,24 @@ def tile_settransform_pa_kernel(tc, set_feats, g0, b0, W0, c0, g1, b1, out):
             with tc.tile_pool(name="result", bufs=3) as result_pool, tc.psum_pool(
                 name="back", bufs=8
             ) as back_pool:
-                for j in range(CHUNKS):
+                def normalise_outputs(j, columns):
                     for block in range(BLOCKS):
                         nc.vector.tensor_scalar(
-                            out=h[j][:, block, :],
-                            in0=h[j][:, block, :],
+                            out=h[j][:, block, columns],
+                            in0=h[j][:, block, columns],
                             scalar1=scale1[:, block : block + 1],
                             scalar2=offset1[:, block : block + 1],
                             op0=ALU.mult,
                             op1=ALU.add,
                         )
+
+                for j in range(CHUNKS):
                     result = result_pool.tile([P, SLICES, D_OUT], F32, name="result")
+                    if j > 0:
+                        normalise_outputs(j, slice(0, CHUNK))
                     for s in range(SLICES):
+                        if j == 0:
+                            normalise_outputs(j, slice(s * P, (s + 1) * P))
                         back = back_pool.tile([P, D_OUT], F32, name="back")
                         for block in range(BLOCKS):
                             nc.tensor.transpose(
@@ -368,6 +392,9 @@ def tile_settransform_pa_kernel(tc, set_feats, g0, b0, W0, c0, g1, b1, out):
                             nc.vector.tensor_copy(out=result[:, s, :], in_=back[:])
                         else:
                             nc.scalar.copy(out=result[:, s, :], in_=back[:])
-                    nc.sync.dma_start(
-                        out=out_rows[:, j * SLICES : (j + 1) * SLICES, :], in_=result[:]
-                    )
+                        if j == 0:
+                            nc.sync.dma_start(out=out_rows[:, s, :], in_=result[:, s, :])
+                    if j > 0:
+                        nc.sync.dma_start(
+                            out=out_rows[:, j * SLICES : (j + 1) * SLICES, :], in_=result[:]
+                        )

@@ -21,9 +21,9 @@ CHUNK = 512
 SLICES = CHUNK // P
 CHUNKS = ROWS // CHUNK
 STATS = 6
+GRAM_COUNTS = [3] * 2 + [2] * 4 + [1] * 10
 GRAM_PLANES = [
-    [(j // 2 + 1) % PACK, (j // 2 + 3) % PACK] if j % 2 == 0 else [(j // 2) % PACK]
-    for j in range(CHUNKS)
+    [(1 + sum(GRAM_COUNTS[:j]) + i) % PACK for i in range(GRAM_COUNTS[j])] for j in range(CHUNKS)
 ]
 GRAM_OF = [[j for j in range(CHUNKS) if t in GRAM_PLANES[j]] for t in range(PACK)]
 VECTOR_OF = [[j for j in range(CHUNKS) if t not in GRAM_PLANES[j]] for t in range(PACK)]
@@ -172,8 +172,8 @@ def tile_settransform_pa_kernel(tc, set_feats, g0, b0, W0, c0, g1, b1, out):
                             identity=ident_bf16[:],
                         )
                     turned = x_turned[:].rearrange("p s n -> p (s n)")
+                    nc.scalar.copy(out=xt[j][:, t, :], in_=turned)
                     if t in GRAM_PLANES[j]:
-                        nc.vector.tensor_copy(out=xt[j][:, t, :], in_=turned)
                         for s in range(SLICES):
                             nc.tensor.matmul(
                                 out=gram[t][:],
@@ -183,7 +183,6 @@ def tile_settransform_pa_kernel(tc, set_feats, g0, b0, W0, c0, g1, b1, out):
                                 stop=(j == GRAM_OF[t][-1] and s == SLICES - 1),
                             )
                     else:
-                        nc.scalar.copy(out=xt[j][:, t, :], in_=turned)
                         at = VECTOR_OF[t].index(j) * STATS
                         nc.vector.bn_stats(
                             out=stats0[:, t, at : at + STATS], in_=xt[j][:, t, :]

@@ -21,15 +21,14 @@ CHUNK = 512
 SLICES = CHUNK // P
 CHUNKS = ROWS // CHUNK
 STATS = 6
-GRAM_COUNTS = [3] * 2 + [2] * 4 + [1] * 10
+GRAM_COUNTS = [2] * 4 + [1] * 12
 GRAM_PLANES = [
     [(1 + sum(GRAM_COUNTS[:j]) + i) % PACK for i in range(GRAM_COUNTS[j])] for j in range(CHUNKS)
 ]
 GRAM_OF = [[j for j in range(CHUNKS) if t in GRAM_PLANES[j]] for t in range(PACK)]
 VECTOR_OF = [[j for j in range(CHUNKS) if t not in GRAM_PLANES[j]] for t in range(PACK)]
-GRAM_ROWS = len(GRAM_OF[0]) * CHUNK
-GRAM_PITCH = D_IN + 16
-GRAM_COLS = P + 1
+GRAM_SIZE = len(GRAM_OF[0])
+GRAM_ROWS = GRAM_SIZE * CHUNK
 WARM_UPS = 5
 CHUNKS_BEFORE_W = 2
 VECTOR_BLOCKS = 2
@@ -39,6 +38,8 @@ PIECES = [(0, slice(0, CHUNK // 2)), (0, slice(CHUNK // 2, CHUNK))] + [
     (j, slice(0, CHUNK)) for j in range(1, CHUNKS)
 ]
 WIDTHS = [columns.stop - columns.start for j, columns in PIECES]
+
+STORE = 2
 
 FLOPS = 2 * ROWS * D_IN * D_OUT
 
@@ -85,6 +86,8 @@ def tile_settransform_pa_kernel(tc, set_feats, g0, b0, W0, c0, g1, b1, out):
         params = keep.tile([P, 5 * BLOCKS], F32, name="params")
         gram_at = len(VECTOR_OF[0]) * STATS
         stats0 = keep.tile([P, BLOCKS, gram_at + 3], F32, name="stats0")
+        gram_sums = keep.tile([P, PACK, GRAM_SIZE], F32, name="gram_sums")
+        gram_total = keep.tile([P, PACK], F32, name="gram_total")
         gram_sq = keep.tile([P, BLOCKS], F32, name="gram_sq")
         gram_mean_sq = keep.tile([P, BLOCKS], F32, name="gram_mean_sq")
         stats1 = keep.tile([P, VECTOR_BLOCKS, CHUNKS, STATS], F32, name="stats1")
@@ -96,12 +99,8 @@ def tile_settransform_pa_kernel(tc, set_feats, g0, b0, W0, c0, g1, b1, out):
         with tc.tile_pool(name="natural", bufs=1) as natural, tc.psum_pool(
             name="turned", bufs=4
         ) as turned_pool, tc.psum_pool(name="gram", bufs=1) as gram_pool:
-            x_nat = []
-            for j in range(CHUNKS):
-                x_tile = natural.tile([P, SLICES, GRAM_PITCH], BF16, name="x_nat%d" % j)
-                nc.gpsimd.memset(x_tile[:, :, D_IN:], 1.0)
-                x_nat.append(x_tile)
-            gram = [gram_pool.tile([P, GRAM_COLS], F32, name="gram%d" % t) for t in range(PACK)]
+            x_nat = [natural.tile([P, SLICES, D_IN], BF16, name="x_nat%d" % j) for j in range(CHUNKS)]
+            gram = [gram_pool.tile([P, P], F32, name="gram%d" % t) for t in range(PACK)]
             diagonal = natural.tile([P, P], F32, name="diagonal")
             nc.vector.memset(stats0[:, :, gram_at : gram_at + 1], float(GRAM_ROWS))
             w_nat = natural.tile([P, BLOCKS, D_IN], BF16, name="w_nat")
@@ -109,7 +108,7 @@ def tile_settransform_pa_kernel(tc, set_feats, g0, b0, W0, c0, g1, b1, out):
                 if j == CHUNKS_BEFORE_W:
                     nc.sync.dma_start(out=w_nat[:], in_=W0.rearrange("(b f) k -> f b k", f=P))
                 nc.sync.dma_start(
-                    out=x_nat[j][:, :, 0:D_IN], in_=x_rows[:, j * SLICES : (j + 1) * SLICES, :]
+                    out=x_nat[j][:], in_=x_rows[:, j * SLICES : (j + 1) * SLICES, :]
                 )
             vec_rows = natural.tile([P, P], BF16, name="vec_rows")
             nc.vector.memset(vec_rows[:], 0.0)
@@ -168,21 +167,28 @@ def tile_settransform_pa_kernel(tc, set_feats, g0, b0, W0, c0, g1, b1, out):
                     for s in range(SLICES):
                         nc.tensor.transpose(
                             out=x_turned[:, s, :],
-                            in_=x_nat[j][:, s, t:D_IN:PACK],
+                            in_=x_nat[j][:, s, t::PACK],
                             identity=ident_bf16[:],
                         )
                     turned = x_turned[:].rearrange("p s n -> p (s n)")
-                    nc.scalar.copy(out=xt[j][:, t, :], in_=turned)
                     if t in GRAM_PLANES[j]:
+                        at = GRAM_OF[t].index(j)
+                        nc.scalar.activation(
+                            out=xt[j][:, t, :],
+                            in_=turned,
+                            func=FUNC.Identity,
+                            accum_out=gram_sums[:, t, at : at + 1],
+                        )
                         for s in range(SLICES):
                             nc.tensor.matmul(
                                 out=gram[t][:],
-                                lhsT=x_nat[j][:, s, t:D_IN:PACK],
-                                rhs=x_nat[j][:, s, t : D_IN + PACK : PACK],
+                                lhsT=x_nat[j][:, s, t::PACK],
+                                rhs=x_nat[j][:, s, t::PACK],
                                 start=(j == GRAM_OF[t][0] and s == 0),
                                 stop=(j == GRAM_OF[t][-1] and s == SLICES - 1),
                             )
                     else:
+                        nc.scalar.copy(out=xt[j][:, t, :], in_=turned)
                         at = VECTOR_OF[t].index(j) * STATS
                         nc.vector.bn_stats(
                             out=stats0[:, t, at : at + STATS], in_=xt[j][:, t, :]
@@ -191,19 +197,16 @@ def tile_settransform_pa_kernel(tc, set_feats, g0, b0, W0, c0, g1, b1, out):
             for t in range(PACK):
                 nc.vector.scalar_tensor_tensor(
                     out=diagonal[:],
-                    in0=gram[t][:, 0:P],
+                    in0=gram[t][:],
                     scalar=1.0,
                     in1=ident_f32[:],
                     op0=ALU.mult,
                     op1=ALU.mult,
                     accum_out=gram_sq[:, t : t + 1],
                 )
-                nc.vector.tensor_scalar_mul(
-                    out=stats0[:, t, gram_at + 1 : gram_at + 2],
-                    in0=gram[t][:, P : P + 1],
-                    scalar1=1.0 / GRAM_ROWS,
-                )
+            nc.vector.reduce_sum(out=gram_total[:], in_=gram_sums[:], axis=mybir.AxisListType.X)
             gram_mean = stats0[:, :, gram_at + 1]
+            nc.vector.tensor_scalar_mul(out=gram_mean, in0=gram_total[:], scalar1=1.0 / GRAM_ROWS)
             nc.vector.tensor_mul(out=gram_mean_sq[:], in0=gram_mean, in1=gram_mean)
             nc.vector.scalar_tensor_tensor(
                 out=stats0[:, :, gram_at + 2],
@@ -359,7 +362,7 @@ def tile_settransform_pa_kernel(tc, set_feats, g0, b0, W0, c0, g1, b1, out):
                 nc, keep, mean_var1, params[:, 3 * BLOCKS : 4 * BLOCKS], params[:, 4 * BLOCKS :], "norm1"
             )
 
-            with tc.tile_pool(name="result", bufs=3) as result_pool, tc.psum_pool(
+            with tc.tile_pool(name="result", bufs=10) as result_pool, tc.psum_pool(
                 name="back", bufs=8
             ) as back_pool:
                 def normalise_outputs(j, columns):
@@ -374,12 +377,13 @@ def tile_settransform_pa_kernel(tc, set_feats, g0, b0, W0, c0, g1, b1, out):
                         )
 
                 for j in range(CHUNKS):
-                    result = result_pool.tile([P, SLICES, D_OUT], F32, name="result")
                     if j > 0:
                         normalise_outputs(j, slice(0, CHUNK))
                     for s in range(SLICES):
                         if j == 0:
                             normalise_outputs(j, slice(s * P, (s + 1) * P))
+                        if s % STORE == 0:
+                            result = result_pool.tile([P, STORE, D_OUT], F32, name="result")
                         back = back_pool.tile([P, D_OUT], F32, name="back")
                         for block in range(BLOCKS):
                             nc.tensor.transpose(
@@ -388,12 +392,9 @@ def tile_settransform_pa_kernel(tc, set_feats, g0, b0, W0, c0, g1, b1, out):
                                 identity=ident_f32[:],
                             )
                         if s == SLICES - 1:
-                            nc.vector.tensor_copy(out=result[:, s, :], in_=back[:])
+                            nc.vector.tensor_copy(out=result[:, s % STORE, :], in_=back[:])
                         else:
-                            nc.scalar.copy(out=result[:, s, :], in_=back[:])
-                        if j == 0:
-                            nc.sync.dma_start(out=out_rows[:, s, :], in_=result[:, s, :])
-                    if j > 0:
-                        nc.sync.dma_start(
-                            out=out_rows[:, j * SLICES : (j + 1) * SLICES, :], in_=result[:]
-                        )
+                            nc.scalar.copy(out=result[:, s % STORE, :], in_=back[:])
+                        if (s + 1) % STORE == 0:
+                            at = j * SLICES + s + 1 - STORE
+                            nc.sync.dma_start(out=out_rows[:, at : at + STORE, :], in_=result[:])

@@ -21,7 +21,7 @@ CHUNK = 512
 SLICES = CHUNK // P
 CHUNKS = ROWS // CHUNK
 STATS = 6
-GRAM_COUNTS = [2] * 4 + [1] * 12
+GRAM_COUNTS = [2, 1] * 6 + [1] * 2 + [0] * 2
 GRAM_PLANES = [
     [(1 + sum(GRAM_COUNTS[:j]) + i) % PACK for i in range(GRAM_COUNTS[j])] for j in range(CHUNKS)
 ]
@@ -123,99 +123,106 @@ def tile_settransform_pa_kernel(tc, set_feats, g0, b0, W0, c0, g1, b1, out):
                     out=in_vecs[v][:], in_=vec.rearrange("(p t) -> p t", t=PACK)
                 )
 
-            warm_up = turned_pool.tile([P, P], F32, tag="turned")
-            for i in range(WARM_UPS):
-                nc.tensor.matmul(
-                    out=warm_up[:], lhsT=ident_f32[:], rhs=ident_f32[:], start=True, stop=True
-                )
-
-            for j in range(CHUNKS):
-                if j == CHUNKS_BEFORE_W:
-                    w_grouped = natural.tile(
-                        [P, D_OUT, PACK], BF16, name="w_grouped", align_bytes=64
-                    )
-                    for block in range(BLOCKS):
-                        w_turned = turned_pool.tile([P, PACK, P], BF16, tag="turned")
-                        for t in range(PACK):
-                            nc.tensor.transpose(
-                                out=w_turned[:, t, :],
-                                in_=w_nat[:, block, t::PACK],
-                                identity=ident_bf16[:],
-                            )
-                        nc.scalar.copy(
-                            out=w_grouped[:, block * P : (block + 1) * P, :],
-                            in_=w_turned[:].rearrange("p t f -> p f t"),
-                        )
-                    nc.vector.quantize_mx(
-                        out=w_codes[:].bitcast(FP8X4),
-                        scales=w_scales[:],
-                        in_=w_grouped[:].rearrange("p f t -> p (f t)"),
-                    )
-                    vec_turned = turned_pool.tile([P, PACK, P], BF16, tag="turned")
-                    nc.tensor.transpose(
-                        out=vec_turned[:, 0, :], in_=vec_rows[:], identity=ident_bf16[:]
-                    )
-                    nc.vector.tensor_copy(
-                        out=params[:, 2 * BLOCKS :], in_=vec_turned[:, 0, 0 : 3 * BLOCKS]
-                    )
-                    for v in range(2):
-                        nc.gpsimd.tensor_copy(
-                            out=params[:, v * BLOCKS : (v + 1) * BLOCKS], in_=in_vecs[v][:]
-                        )
-                for t in range(PACK):
-                    x_turned = turned_pool.tile([P, SLICES, P], BF16, tag="turned")
-                    for s in range(SLICES):
+            def turn_weights():
+                for block in range(BLOCKS):
+                    w_turned = turned_pool.tile([P, PACK, P], BF16, tag="turned")
+                    for t in range(PACK):
                         nc.tensor.transpose(
-                            out=x_turned[:, s, :],
-                            in_=x_nat[j][:, s, t::PACK],
+                            out=w_turned[:, t, :],
+                            in_=w_nat[:, block, t::PACK],
                             identity=ident_bf16[:],
                         )
-                    turned = x_turned[:].rearrange("p s n -> p (s n)")
-                    if t in GRAM_PLANES[j]:
-                        at = GRAM_OF[t].index(j)
-                        nc.scalar.activation(
-                            out=xt[j][:, t, :],
-                            in_=turned,
-                            func=FUNC.Identity,
-                            accum_out=gram_sums[:, t, at : at + 1],
-                        )
-                        for s in range(SLICES):
-                            nc.tensor.matmul(
-                                out=gram[t][:],
-                                lhsT=x_nat[j][:, s, t::PACK],
-                                rhs=x_nat[j][:, s, t::PACK],
-                                start=(j == GRAM_OF[t][0] and s == 0),
-                                stop=(j == GRAM_OF[t][-1] and s == SLICES - 1),
-                            )
-                    else:
-                        nc.scalar.copy(out=xt[j][:, t, :], in_=turned)
-                        at = VECTOR_OF[t].index(j) * STATS
-                        nc.vector.bn_stats(
-                            out=stats0[:, t, at : at + STATS], in_=xt[j][:, t, :]
-                        )
+                    nc.scalar.copy(
+                        out=w_grouped[:, block * P : (block + 1) * P, :],
+                        in_=w_turned[:].rearrange("p t f -> p f t"),
+                    )
 
-            for t in range(PACK):
-                nc.vector.scalar_tensor_tensor(
-                    out=diagonal[:],
-                    in0=gram[t][:],
-                    scalar=1.0,
-                    in1=ident_f32[:],
-                    op0=ALU.mult,
-                    op1=ALU.mult,
-                    accum_out=gram_sq[:, t : t + 1],
+            def finish_constants():
+                nc.vector.quantize_mx(
+                    out=w_codes[:].bitcast(FP8X4),
+                    scales=w_scales[:],
+                    in_=w_grouped[:].rearrange("p f t -> p (f t)"),
                 )
-            nc.vector.reduce_sum(out=gram_total[:], in_=gram_sums[:], axis=mybir.AxisListType.X)
-            gram_mean = stats0[:, :, gram_at + 1]
-            nc.vector.tensor_scalar_mul(out=gram_mean, in0=gram_total[:], scalar1=1.0 / GRAM_ROWS)
-            nc.vector.tensor_mul(out=gram_mean_sq[:], in0=gram_mean, in1=gram_mean)
-            nc.vector.scalar_tensor_tensor(
-                out=stats0[:, :, gram_at + 2],
-                in0=gram_mean_sq[:],
-                scalar=-float(GRAM_ROWS),
-                in1=gram_sq[:],
-                op0=ALU.mult,
-                op1=ALU.add,
-            )
+                vec_turned = turned_pool.tile([P, PACK, P], BF16, tag="turned")
+                nc.tensor.transpose(
+                    out=vec_turned[:, 0, :], in_=vec_rows[:], identity=ident_bf16[:]
+                )
+                nc.scalar.copy(out=params[:, 2 * BLOCKS :], in_=vec_turned[:, 0, 0 : 3 * BLOCKS])
+                for v in range(2):
+                    nc.gpsimd.tensor_copy(
+                        out=params[:, v * BLOCKS : (v + 1) * BLOCKS], in_=in_vecs[v][:]
+                    )
+
+            def turn_plane(j, t):
+                x_turned = turned_pool.tile([P, SLICES, P], BF16, tag="turned")
+                for s in range(SLICES):
+                    nc.tensor.transpose(
+                        out=x_turned[:, s, :],
+                        in_=x_nat[j][:, s, t::PACK],
+                        identity=ident_bf16[:],
+                    )
+                turned = x_turned[:].rearrange("p s n -> p (s n)")
+                if t in GRAM_PLANES[j]:
+                    at = GRAM_OF[t].index(j)
+                    nc.scalar.activation(
+                        out=xt[j][:, t, :],
+                        in_=turned,
+                        func=FUNC.Identity,
+                        accum_out=gram_sums[:, t, at : at + 1],
+                    )
+                    for s in range(SLICES):
+                        nc.tensor.matmul(
+                            out=gram[t][:],
+                            lhsT=x_nat[j][:, s, t::PACK],
+                            rhs=x_nat[j][:, s, t::PACK],
+                            start=(j == GRAM_OF[t][0] and s == 0),
+                            stop=(j == GRAM_OF[t][-1] and s == SLICES - 1),
+                        )
+                else:
+                    nc.scalar.copy(out=xt[j][:, t, :], in_=turned)
+                    at = VECTOR_OF[t].index(j) * STATS
+                    nc.vector.bn_stats(out=stats0[:, t, at : at + STATS], in_=xt[j][:, t, :])
+
+            def finish_gram():
+                for t in range(PACK):
+                    nc.vector.scalar_tensor_tensor(
+                        out=diagonal[:],
+                        in0=gram[t][:],
+                        scalar=1.0,
+                        in1=ident_f32[:],
+                        op0=ALU.mult,
+                        op1=ALU.mult,
+                        accum_out=gram_sq[:, t : t + 1],
+                    )
+                nc.vector.reduce_sum(out=gram_total[:], in_=gram_sums[:], axis=mybir.AxisListType.X)
+                gram_mean = stats0[:, :, gram_at + 1]
+                nc.vector.tensor_scalar_mul(out=gram_mean, in0=gram_total[:], scalar1=1.0 / GRAM_ROWS)
+                nc.vector.tensor_mul(out=gram_mean_sq[:], in0=gram_mean, in1=gram_mean)
+                nc.vector.scalar_tensor_tensor(
+                    out=stats0[:, :, gram_at + 2],
+                    in0=gram_mean_sq[:],
+                    scalar=-float(GRAM_ROWS),
+                    in1=gram_sq[:],
+                    op0=ALU.mult,
+                    op1=ALU.add,
+                )
+
+            w_grouped = natural.tile([P, D_OUT, PACK], BF16, name="w_grouped", align_bytes=64)
+            with tc.manual_schedule():
+                warm_up = turned_pool.tile([P, P], F32, tag="turned")
+                for i in range(WARM_UPS):
+                    nc.tensor.matmul(
+                        out=warm_up[:], lhsT=ident_f32[:], rhs=ident_f32[:], start=True, stop=True
+                    )
+                for j in range(CHUNKS):
+                    if j == CHUNKS_BEFORE_W:
+                        turn_weights()
+                    if j == CHUNKS_BEFORE_W + 2:
+                        finish_constants()
+                    if j == CHUNKS - 1:
+                        finish_gram()
+                    for t in range(PACK):
+                        turn_plane(j, t)
 
         mean_var0 = keep.tile([P, BLOCKS, 2], F32, name="mean_var0")
         for t in range(PACK):
@@ -382,7 +389,8 @@ def tile_settransform_pa_kernel(tc, set_feats, g0, b0, W0, c0, g1, b1, out):
                     for s in range(SLICES):
                         if j == 0:
                             normalise_outputs(j, slice(s * P, (s + 1) * P))
-                        if s % STORE == 0:
+                        store = 1 if j == 0 else STORE
+                        if s % store == 0:
                             result = result_pool.tile([P, STORE, D_OUT], F32, name="result")
                         back = back_pool.tile([P, D_OUT], F32, name="back")
                         for block in range(BLOCKS):
@@ -392,9 +400,11 @@ def tile_settransform_pa_kernel(tc, set_feats, g0, b0, W0, c0, g1, b1, out):
                                 identity=ident_f32[:],
                             )
                         if s == SLICES - 1:
-                            nc.vector.tensor_copy(out=result[:, s % STORE, :], in_=back[:])
+                            nc.vector.tensor_copy(out=result[:, s % store, :], in_=back[:])
                         else:
-                            nc.scalar.copy(out=result[:, s % STORE, :], in_=back[:])
-                        if (s + 1) % STORE == 0:
-                            at = j * SLICES + s + 1 - STORE
-                            nc.sync.dma_start(out=out_rows[:, at : at + STORE, :], in_=result[:])
+                            nc.scalar.copy(out=result[:, s % store, :], in_=back[:])
+                        if (s + 1) % store == 0:
+                            at = j * SLICES + s + 1 - store
+                            nc.sync.dma_start(
+                                out=out_rows[:, at : at + store, :], in_=result[:, 0:store, :]
+                            )

import concourse.mybir as mybir
from concourse.masks import make_identity

F32 = mybir.dt.float32
BF16 = mybir.dt.bfloat16
U32 = mybir.dt.uint32
U8 = mybir.dt.uint8
FP8X4 = mybir.dt.float8_e4m3fn_x4
ALU = mybir.AluOpType
FUNC = mybir.ActivationFunctionType

P = 128
PACK = 4
ROWS = 64 * 128
D_IN = 512
D_OUT = 512
EPS = 1e-5
BLOCKS = 4
ROWS_PER_PARTITION = ROWS // P
CHUNK = 512
SLICES = CHUNK // P
CHUNKS = ROWS // CHUNK
STATS = 6
GRAM_COUNTS = [2, 1] * 6 + [1] * 2 + [0] * 2
GRAM_PLANES = [
    [(1 + sum(GRAM_COUNTS[:j]) + i) % PACK for i in range(GRAM_COUNTS[j])] for j in range(CHUNKS)
]
GRAM_OF = [[j for j in range(CHUNKS) if t in GRAM_PLANES[j]] for t in range(PACK)]
VECTOR_OF = [[j for j in range(CHUNKS) if t not in GRAM_PLANES[j]] for t in range(PACK)]
GRAM_SIZE = len(GRAM_OF[0])
GRAM_ROWS = GRAM_SIZE * CHUNK
WARM_UPS = 5
CHUNKS_BEFORE_W = 2
VECTOR_BLOCKS = 2
SCALAR_BLOCKS = BLOCKS - VECTOR_BLOCKS
LAG = 2
PIECES = [(0, slice(0, CHUNK // 2)), (0, slice(CHUNK // 2, CHUNK))] + [
    (j, slice(0, CHUNK)) for j in range(1, CHUNKS)
]
WIDTHS = [columns.stop - columns.start for j, columns in PIECES]

STORE = 2

FLOPS = 2 * ROWS * D_IN * D_OUT


def norm_coefficients(nc, pool, mean_var, gain, shift, label):
    rstd = pool.tile([P, BLOCKS], F32, name=label + "_rstd")
    nc.scalar.activation(
        out=rstd[:], in_=mean_var[:, :, 1], func=FUNC.Abs_reciprocal_sqrt, bias=EPS
    )
    var_eps = pool.tile([P, BLOCKS], F32, name=label + "_var_eps")
    nc.vector.tensor_scalar_add(out=var_eps[:], in0=mean_var[:, :, 1], scalar1=EPS)
    newton = pool.tile([P, BLOCKS], F32, name=label + "_newton")
    nc.vector.tensor_mul(out=newton[:], in0=rstd[:], in1=rstd[:])
    scale = pool.tile([P, BLOCKS], F32, name=label + "_scale")
    nc.vector.tensor_mul(out=scale[:], in0=rstd[:], in1=gain)
    nc.vector.scalar_tensor_tensor(
        out=newton[:], in0=newton[:], scalar=-0.5, in1=var_eps[:], op0=ALU.mult, op1=ALU.mult
    )
    nc.vector.scalar_tensor_tensor(
        out=scale[:], in0=newton[:], scalar=1.5, in1=scale[:], op0=ALU.add, op1=ALU.mult
    )
    offset = pool.tile([P, BLOCKS], F32, name=label + "_offset")
    nc.vector.tensor_mul(out=offset[:], in0=mean_var[:, :, 0], in1=scale[:])
    nc.vector.tensor_sub(out=offset[:], in0=shift, in1=offset[:])
    return scale, offset


def tile_settransform_pa_kernel(tc, set_feats, g0, b0, W0, c0, g1, b1, out):
    nc = tc.nc
    x_rows = set_feats.flatten_outer_dims().rearrange("(p c) k -> p c k", c=ROWS_PER_PARTITION)
    out_rows = out.flatten_outer_dims().rearrange("(p c) f -> p c f", c=ROWS_PER_PARTITION)

    with tc.tile_pool(name="keep", bufs=1) as keep:
        ident_bf16 = keep.tile([P, P], BF16, name="ident_bf16")
        make_identity(nc, ident_bf16[:])
        ident_f32 = keep.tile([P, P], F32, name="ident_f32")
        make_identity(nc, ident_f32[:])
        warm = keep.tile([P, 1], F32, name="warm")
        nc.vector.memset(warm[:], 1.0)
        nc.scalar.activation(out=warm[:], in_=warm[:], func=FUNC.Abs_reciprocal_sqrt)

        w_codes = keep.tile([P, D_OUT], U32, name="w_codes", align_bytes=64)
        w_scales = keep.tile([P, D_OUT], U8, name="w_scales", align_bytes=64)
        params = keep.tile([P, 5 * BLOCKS], F32, name="params")
        gram_at = len(VECTOR_OF[0]) * STATS
        stats0 = keep.tile([P, BLOCKS, gram_at + 3], F32, name="stats0")
        gram_sums = keep.tile([P, PACK, GRAM_SIZE], F32, name="gram_sums")
        gram_total = keep.tile([P, PACK], F32, name="gram_total")
        gram_sq = keep.tile([P, BLOCKS], F32, name="gram_sq")
        gram_mean_sq = keep.tile([P, BLOCKS], F32, name="gram_mean_sq")
        stats1 = keep.tile([P, VECTOR_BLOCKS, CHUNKS, STATS], F32, name="stats1")
        sum_h = keep.tile([P, SCALAR_BLOCKS, len(PIECES)], F32, name="sum_h")
        sum_sq = keep.tile([P, SCALAR_BLOCKS, CHUNKS], F32, name="sum_sq")
        neg_shift = keep.tile([P, SCALAR_BLOCKS], F32, name="neg_shift")
        xt = [keep.tile([P, BLOCKS, CHUNK], BF16, name="xt%d" % j) for j in range(CHUNKS)]

        with tc.tile_pool(name="natural", bufs=1) as natural, tc.psum_pool(
            name="turned", bufs=4
        ) as turned_pool, tc.psum_pool(name="gram", bufs=1) as gram_pool:
            x_nat = [natural.tile([P, SLICES, D_IN], BF16, name="x_nat%d" % j) for j in range(CHUNKS)]
            gram = [gram_pool.tile([P, P], F32, name="gram%d" % t) for t in range(PACK)]
            diagonal = natural.tile([P, P], F32, name="diagonal")
            nc.vector.memset(stats0[:, :, gram_at : gram_at + 1], float(GRAM_ROWS))
            w_nat = natural.tile([P, BLOCKS, D_IN], BF16, name="w_nat")
            for j in range(CHUNKS):
                if j == CHUNKS_BEFORE_W:
                    nc.sync.dma_start(out=w_nat[:], in_=W0.rearrange("(b f) k -> f b k", f=P))
                nc.sync.dma_start(
                    out=x_nat[j][:], in_=x_rows[:, j * SLICES : (j + 1) * SLICES, :]
                )
            vec_rows = natural.tile([P, P], BF16, name="vec_rows")
            nc.vector.memset(vec_rows[:], 0.0)
            for v, vec in enumerate((c0, g1, b1)):
                nc.scalar.dma_start(
                    out=vec_rows[BLOCKS * v : BLOCKS * (v + 1), :],
                    in_=vec.rearrange("(t p) -> t p", p=P),
                )
            in_vecs = [natural.tile([P, PACK], BF16, name="in_vec%d" % v) for v in range(2)]
            for v, vec in enumerate((g0, b0)):
                nc.scalar.dma_start(
                    out=in_vecs[v][:], in_=vec.rearrange("(p t) -> p t", t=PACK)
                )

            def turn_weights():
                for block in range(BLOCKS):
                    w_turned = turned_pool.tile([P, PACK, P], BF16, tag="turned")
                    for t in range(PACK):
                        nc.tensor.transpose(
                            out=w_turned[:, t, :],
                            in_=w_nat[:, block, t::PACK],
                            identity=ident_bf16[:],
                        )
                    nc.scalar.copy(
                        out=w_grouped[:, block * P : (block + 1) * P, :],
                        in_=w_turned[:].rearrange("p t f -> p f t"),
                    )

            def finish_constants():
                nc.vector.quantize_mx(
                    out=w_codes[:].bitcast(FP8X4),
                    scales=w_scales[:],
                    in_=w_grouped[:].rearrange("p f t -> p (f t)"),
                )
                vec_turned = turned_pool.tile([P, PACK, P], BF16, tag="turned")
                nc.tensor.transpose(
                    out=vec_turned[:, 0, :], in_=vec_rows[:], identity=ident_bf16[:]
                )
                nc.scalar.copy(out=params[:, 2 * BLOCKS :], in_=vec_turned[:, 0, 0 : 3 * BLOCKS])
                for v in range(2):
                    nc.gpsimd.tensor_copy(
                        out=params[:, v * BLOCKS : (v + 1) * BLOCKS], in_=in_vecs[v][:]
                    )

            def turn_plane(j, t):
                x_turned = turned_pool.tile([P, SLICES, P], BF16, tag="turned")
                for s in range(SLICES):
                    nc.tensor.transpose(
                        out=x_turned[:, s, :],
                        in_=x_nat[j][:, s, t::PACK],
                        identity=ident_bf16[:],
                    )
                turned = x_turned[:].rearrange("p s n -> p (s n)")
                if t in GRAM_PLANES[j]:
                    at = GRAM_OF[t].index(j)
                    nc.scalar.activation(
                        out=xt[j][:, t, :],
                        in_=turned,
                        func=FUNC.Identity,
                        accum_out=gram_sums[:, t, at : at + 1],
                    )
                    for s in range(SLICES):
                        nc.tensor.matmul(
                            out=gram[t][:],
                            lhsT=x_nat[j][:, s, t::PACK],
                            rhs=x_nat[j][:, s, t::PACK],
                            start=(j == GRAM_OF[t][0] and s == 0),
                            stop=(j == GRAM_OF[t][-1] and s == SLICES - 1),
                        )
                else:
                    nc.scalar.copy(out=xt[j][:, t, :], in_=turned)
                    at = VECTOR_OF[t].index(j) * STATS
                    nc.vector.bn_stats(out=stats0[:, t, at : at + STATS], in_=xt[j][:, t, :])

            def finish_gram():
                for t in range(PACK):
                    nc.vector.scalar_tensor_tensor(
                        out=diagonal[:],
                        in0=gram[t][:],
                        scalar=1.0,
                        in1=ident_f32[:],
                        op0=ALU.mult,
                        op1=ALU.mult,
                        accum_out=gram_sq[:, t : t + 1],
                    )
                nc.vector.reduce_sum(out=gram_total[:], in_=gram_sums[:], axis=mybir.AxisListType.X)
                gram_mean = stats0[:, :, gram_at + 1]
                nc.vector.tensor_scalar_mul(out=gram_mean, in0=gram_total[:], scalar1=1.0 / GRAM_ROWS)
                nc.vector.tensor_mul(out=gram_mean_sq[:], in0=gram_mean, in1=gram_mean)
                nc.vector.scalar_tensor_tensor(
                    out=stats0[:, :, gram_at + 2],
                    in0=gram_mean_sq[:],
                    scalar=-float(GRAM_ROWS),
                    in1=gram_sq[:],
                    op0=ALU.mult,
                    op1=ALU.add,
                )

            w_grouped = natural.tile([P, D_OUT, PACK], BF16, name="w_grouped", align_bytes=64)
            with tc.manual_schedule():
                warm_up = turned_pool.tile([P, P], F32, tag="turned")
                for i in range(WARM_UPS):
                    nc.tensor.matmul(
                        out=warm_up[:], lhsT=ident_f32[:], rhs=ident_f32[:], start=True, stop=True
                    )
                for j in range(CHUNKS):
                    if j == CHUNKS_BEFORE_W:
                        turn_weights()
                    if j == CHUNKS_BEFORE_W + 2:
                        finish_constants()
                    if j == CHUNKS - 1:
                        finish_gram()
                    for t in range(PACK):
                        turn_plane(j, t)

        mean_var0 = keep.tile([P, BLOCKS, 2], F32, name="mean_var0")
        for t in range(PACK):
            nc.vector.bn_aggr(
                out=mean_var0[:, t, :], in_=stats0[:, t, :]
            )
        scale0, offset0 = norm_coefficients(
            nc, keep, mean_var0, params[:, 0:BLOCKS], params[:, BLOCKS : 2 * BLOCKS], "norm0"
        )
        bias = params[:, 2 * BLOCKS : 3 * BLOCKS]

        with tc.tile_pool(name="hidden", bufs=1) as hidden:
            h = [hidden.tile([P, BLOCKS, CHUNK], F32, name="h%d" % j) for j in range(CHUNKS)]

            with tc.tile_pool(name="operand", bufs=3) as operand, tc.psum_pool(
                name="sums", bufs=8
            ) as sums_pool:
                codes, scales, grouped = {}, {}, {}

                def normalise(i):
                    j, columns = PIECES[i]
                    for t in range(PACK):
                        nc.vector.tensor_scalar(
                            out=xt[j][:, t, columns],
                            in0=xt[j][:, t, columns],
                            scalar1=scale0[:, t : t + 1],
                            scalar2=offset0[:, t : t + 1],
                            op0=ALU.mult,
                            op1=ALU.add,
                        )

                def interleave(i):
                    j, columns = PIECES[i]
                    grouped[i] = operand.tile(
                        [P, CHUNK, PACK], BF16, name="grouped", align_bytes=64
                    )
                    nc.vector.tensor_copy(
                        out=grouped[i][:, 0 : WIDTHS[i], :].rearrange("p (c i) t -> p c t i", i=4),
                        in_=xt[j][:, :, columns].rearrange("p t (c i) -> p c t i", i=4),
                    )

                def quantise(i):
                    codes[i] = operand.tile([P, CHUNK], U32, name="codes", align_bytes=64)
                    scales[i] = operand.tile([P, CHUNK], U8, name="scales", align_bytes=64)
                    nc.vector.quantize_mx(
                        out=codes[i][:, 0 : WIDTHS[i]].bitcast(FP8X4),
                        scales=scales[i][:, 0 : WIDTHS[i]],
                        in_=grouped[i][:, 0 : WIDTHS[i], :].rearrange("p n t -> p (n t)"),
                    )

                def multiply(i):
                    j, columns = PIECES[i]
                    for block in range(BLOCKS):
                        features = slice(block * P, (block + 1) * P)
                        sums = sums_pool.tile([P, CHUNK], F32, name="sums")
                        nc.tensor.matmul_mx(
                            out=sums[:, 0 : WIDTHS[i]],
                            lhsT=w_codes[:, features].bitcast(FP8X4),
                            lhsT_scale=w_scales[:, features],
                            rhs=codes[i][:, 0 : WIDTHS[i]].bitcast(FP8X4),
                            rhs_scale=scales[i][:, 0 : WIDTHS[i]],
                            start=True,
                            stop=True,
                        )
                        if block < VECTOR_BLOCKS:
                            nc.scalar.activation(
                                out=h[j][:, block, columns],
                                in_=sums[:, 0 : WIDTHS[i]],
                                func=FUNC.Relu,
                                bias=bias[:, block : block + 1],
                            )
                        else:
                            nc.scalar.activation(
                                out=h[j][:, block, columns],
                                in_=sums[:, 0 : WIDTHS[i]],
                                func=FUNC.Relu,
                                bias=bias[:, block : block + 1],
                                accum_out=sum_h[:, block - VECTOR_BLOCKS, i : i + 1],
                            )
                    if i == 0:
                        nc.scalar.mul(out=neg_shift[:], in_=sum_h[:, :, 0], mul=-1.0 / WIDTHS[0])
                    if columns.stop == CHUNK:
                        for b in range(SCALAR_BLOCKS):
                            squares = operand.tile([P, CHUNK], F32, name="squares")
                            nc.scalar.activation(
                                out=squares[:],
                                in_=h[j][:, VECTOR_BLOCKS + b, :],
                                func=FUNC.Square,
                                bias=neg_shift[:, b : b + 1],
                                accum_out=sum_sq[:, b, j : j + 1],
                            )

                def measure(i, block):
                    j, columns = PIECES[i]
                    if columns.stop == CHUNK:
                        nc.vector.bn_stats(out=stats1[:, block, j, :], in_=h[j][:, block, :])

                with tc.manual_schedule():
                    normalise(0)
                    for i in range(len(PIECES) + LAG):
                        if i < len(PIECES):
                            interleave(i)
                        if i >= LAG:
                            measure(i - LAG, 0)
                        if i < len(PIECES):
                            quantise(i)
                            multiply(i)
                        if i + 1 < len(PIECES):
                            normalise(i + 1)
                        if i >= LAG:
                            measure(i - LAG, 1)

            mean_var1 = keep.tile([P, BLOCKS, 2], F32, name="mean_var1")
            for block in range(VECTOR_BLOCKS):
                nc.vector.bn_aggr(
                    out=mean_var1[:, block, :],
                    in_=stats1[:, block, :, :].rearrange("p j s -> p (j s)"),
                )
            scalar_mean = mean_var1[:, VECTOR_BLOCKS:, 0]
            total_h = keep.tile([P, SCALAR_BLOCKS], F32, name="total_h")
            nc.vector.reduce_sum(out=total_h[:], in_=sum_h[:], axis=mybir.AxisListType.X)
            total_sq = keep.tile([P, SCALAR_BLOCKS], F32, name="total_sq")
            nc.vector.reduce_sum(out=total_sq[:], in_=sum_sq[:], axis=mybir.AxisListType.X)
            gap = keep.tile([P, SCALAR_BLOCKS], F32, name="gap")
            nc.vector.scalar_tensor_tensor(
                out=gap[:],
                in0=total_h[:],
                scalar=1.0 / ROWS,
                in1=neg_shift[:],
                op0=ALU.mult,
                op1=ALU.add,
            )
            nc.vector.tensor_scalar_mul(out=scalar_mean, in0=total_h[:], scalar1=1.0 / ROWS)
            nc.vector.tensor_mul(out=gap[:], in0=gap[:], in1=gap[:])
            nc.vector.scalar_tensor_tensor(
                out=mean_var1[:, VECTOR_BLOCKS:, 1],
                in0=total_sq[:],
                scalar=1.0 / ROWS,
                in1=gap[:],
                op0=ALU.mult,
                op1=ALU.subtract,
            )
            scale1, offset1 = norm_coefficients(
                nc, keep, mean_var1, params[:, 3 * BLOCKS : 4 * BLOCKS], params[:, 4 * BLOCKS :], "norm1"
            )

            with tc.tile_pool(name="result", bufs=10) as result_pool, tc.psum_pool(
                name="back", bufs=8
            ) as back_pool:
                def normalise_outputs(j, columns):
                    for block in range(BLOCKS):
                        nc.vector.tensor_scalar(
                            out=h[j][:, block, columns],
                            in0=h[j][:, block, columns],
                            scalar1=scale1[:, block : block + 1],
                            scalar2=offset1[:, block : block + 1],
                            op0=ALU.mult,
                            op1=ALU.add,
                        )

                for j in range(CHUNKS):
                    if j > 0:
                        normalise_outputs(j, slice(0, CHUNK))
                    for s in range(SLICES):
                        if j == 0:
                            normalise_outputs(j, slice(s * P, (s + 1) * P))
                        store = 1 if j == 0 else STORE
                        if s % store == 0:
                            result = result_pool.tile([P, STORE, D_OUT], F32, name="result")
                        back = back_pool.tile([P, D_OUT], F32, name="back")
                        for block in range(BLOCKS):
                            nc.tensor.transpose(
                                out=back[:, block * P : (block + 1) * P],
                                in_=h[j][:, block, s * P : (s + 1) * P],
                                identity=ident_f32[:],
                            )
                        if s == SLICES - 1:
                            nc.vector.tensor_copy(out=result[:, s % store, :], in_=back[:])
                        else:
                            nc.scalar.copy(out=result[:, s % store, :], in_=back[:])
                        if (s + 1) % store == 0:
                            at = j * SLICES + s + 1 - store
                            nc.sync.dma_start(
                                out=out_rows[:, at : at + store, :], in_=result[:, 0:store, :]
                            )
